import numpy as np
import ml_dtypes

BF16 = ml_dtypes.bfloat16


def bf(x):
    return np.asarray(x, np.float32).astype(BF16)


def f32(x):
    return np.asarray(x, np.float32)


def f64(x):
    return np.asarray(x).astype(np.float64)


def striped(idx):
    return np.tile(idx.reshape(-1, 16).T, (8, 1))


C, S, N = 256, 2048, 512
EPS = 1e-6


def setup_inputs():
    return {"emb": f32(np.random.standard_normal((C, S))), "q": f32(np.random.standard_normal((C, N))), "k": f32(np.random.standard_normal((C, N))), "v": f32(np.random.standard_normal((C, N))), "offs": striped(np.random.permutation(S)[:N])}


def reference(emb, q, k, v, offs):
    idx = offs[:16].T.reshape(-1)
    e = f64(emb)[:, idx]
    qe = e + f64(q)
    ke = e + f64(k)
    ve = e + f64(v)
    s = qe.T @ ke / np.sqrt(C)
    mu = s.mean(axis=1, keepdims=True)
    sd = np.sqrt(((s - mu) ** 2).sum(axis=1, keepdims=True) / (N - 1))
    z = (s - mu) / (sd + EPS)
    p = np.exp(z - z.max(axis=1, keepdims=True))
    p = p / p.sum(axis=1, keepdims=True)
    return ve @ p.T

@@ -1,0 +1,112 @@
+import math
+
+import concourse.mybir as mybir
+from concourse.masks import make_identity
+
+P = 128
+C, S, N = 256, 2048, 512
+CB = C // P
+NB = N // P
+EPS = 1e-6
+
+FLOPS = 2 * 2 * N * N * C
+BYTES = 4 * (C * N + 3 * C * N + C * N) + 2 * P * (N // 16)
+
+F32, BF16, U16 = mybir.dt.float32, mybir.dt.bfloat16, mybir.dt.uint16
+ADD, MULT, POW = mybir.AluOpType.add, mybir.AluOpType.mult, mybir.AluOpType.pow
+EXP = mybir.ActivationFunctionType.Exp
+
+
+def tile_neuromodulatedattentionwithelectrodes_kernel(tc, emb, q, k, v, offs, out):
+    nc = tc.nc
+    with (
+        tc.tile_pool(name="held", bufs=1) as held,
+        tc.tile_pool(name="rows", bufs=2) as rows,
+        tc.tile_pool(name="small", bufs=4) as small,
+        tc.psum_pool(name="scores", bufs=NB) as scores,
+        tc.psum_pool(name="flipped", bufs=2) as flipped,
+        tc.psum_pool(name="products", bufs=2) as products,
+    ):
+        offsets = held.tile([P, N // 16], U16, name="offsets")
+        nc.sync.dma_start(offsets[:], offs)
+        table = [held.tile([P, S], F32, name=f"table{cb}") for cb in range(CB)]
+        plain = {
+            (name, cb): held.tile([P, N], F32, name=f"{name}{cb}") for name in "kqv" for cb in range(CB)
+        }
+        for cb in range(CB):
+            channels = slice(cb * P, (cb + 1) * P)
+            nc.sync.dma_start(table[cb][:], emb[channels, :])
+            for name, source in (("k", k), ("q", q), ("v", v)):
+                nc.sync.dma_start(plain[name, cb][:], source[channels, :])
+
+        identity32 = held.tile([P, P], F32, name="identity32")
+        make_identity(nc, identity32[:])
+        identity16 = held.tile([P, P], BF16, name="identity16")
+        make_identity(nc, identity16[:])
+        half = held.tile([P, 1], F32, name="half")
+        nc.gpsimd.memset(half[:], 0.5)
+        warm = held.tile([P, 1], F32, name="warm")
+        nc.scalar.activation(warm[:], half[:], EXP)
+
+        summed = {}
+        rounded = {}
+        s_ps = [scores.tile([P, N], F32, name=f"s_ps{jb}", tag="s_ps") for jb in range(NB)]
+        for cb in range(CB):
+            for name in "kqv":
+                summed[name, cb] = held.tile([P, N], F32, name=f"{name}e32_{cb}")
+                nc.vector.tensor_tensor(
+                    summed[name, cb][:], table[cb][:].indirect(offsets[:]), plain[name, cb][:], ADD
+                )
+            for name in "kq":
+                rounded[name, cb] = held.tile([P, N], BF16, name=f"{name}e16_{cb}")
+                nc.scalar.copy(rounded[name, cb][:], summed[name, cb][:])
+            for jb in range(NB):
+                nc.tensor.matmul(
+                    s_ps[jb][:],
+                    rounded["q", cb][:, jb * P : (jb + 1) * P],
+                    rounded["k", cb][:],
+                    start=(cb == 0),
+                    stop=(cb == CB - 1),
+                )
+
+        veT = []
+        for cb in range(CB):
+            veT_ps = flipped.tile([P, NB, P], F32, name="veT_ps", tag="flip")
+            for ib in range(NB):
+                nc.tensor.transpose(veT_ps[:, ib, :], summed["v", cb][:, ib * P : (ib + 1) * P], identity32[:])
+            veT.append(held.tile([P, NB, P], BF16, name=f"veT{cb}"))
+            nc.scalar.copy(veT[cb][:], veT_ps[:])
+
+        out_blocks = out.rearrange("(cb p) j -> p cb j", p=P)
+        for jb in range(NB):
+            stats = small.tile([P, 6], F32, name="stats")
+            nc.vector.bn_stats(stats[:], s_ps[jb][:])
+            mean_var = small.tile([P, 2], F32, name="mean_var")
+            nc.vector.bn_aggr(mean_var[:], stats[:])
+            root = small.tile([P, 1], F32, name="root")
+            nc.gpsimd.tensor_tensor(root[:], mean_var[:, 1:2], half[:], POW)
+            gain = small.tile([P, 1], F32, name="gain")
+            nc.vector.tensor_scalar(gain[:], root[:], math.sqrt(N / (N - 1)), math.sqrt(C) * EPS, MULT, ADD)
+            nc.vector.reciprocal(gain[:], gain[:])
+            shift = small.tile([P, 1], F32, name="shift")
+            nc.vector.tensor_scalar(shift[:], mean_var[:, 0:1], gain[:], -1.0, MULT, MULT)
+            e = rows.tile([P, N], F32, name="e")
+            e_sum = small.tile([P, 1], F32, name="e_sum")
+            nc.scalar.activation(e[:], s_ps[jb][:], EXP, bias=shift[:], scale=gain[:], accum_out=e_sum[:])
+            nc.vector.reciprocal(e_sum[:], e_sum[:])
+            p = rows.tile([P, N], BF16, name="p")
+            nc.vector.tensor_scalar(p[:], e[:], e_sum[:], None, MULT)
+            pT_ps = flipped.tile([P, NB, P], BF16, name="pT_ps", tag="flip")
+            for ib in range(NB):
+                nc.tensor.transpose(pT_ps[:, ib, :], p[:, ib * P : (ib + 1) * P], identity16[:])
+            pT = rows.tile([P, NB, P], BF16, name="pT")
+            nc.scalar.copy(pT[:], pT_ps[:])
+            o_ps = products.tile([P, CB, P], F32, name="o_ps")
+            for cb in range(CB):
+                for ib in range(NB):
+                    nc.tensor.matmul(
+                        o_ps[:, cb, :], veT[cb][:, ib, :], pT[:, ib, :], start=(ib == 0), stop=(ib == NB - 1)
+                    )
+            o = rows.tile([P, CB, P], F32, name="o")
+            nc.scalar.copy(o[:], o_ps[:])
+            nc.sync.dma_start(out_blocks[:, :, jb * P : (jb + 1) * P], o[:])

@@ -21,8 +21,6 @@ def tile_neuromodulatedattentionwithelectrodes_kernel(tc, emb, q, k, v, offs, ou
     nc = tc.nc
     with (
         tc.tile_pool(name="held", bufs=1) as held,
-        tc.tile_pool(name="rows", bufs=2) as rows,
-        tc.tile_pool(name="small", bufs=4) as small,
         tc.psum_pool(name="scores", bufs=NB) as scores,
         tc.psum_pool(name="flipped", bufs=2) as flipped,
         tc.psum_pool(name="products", bufs=2) as products,
@@ -50,6 +48,7 @@ def tile_neuromodulatedattentionwithelectrodes_kernel(tc, emb, q, k, v, offs, ou
 
         summed = {}
         rounded = {}
+        veT = []
         s_ps = [scores.tile([P, N], F32, name=f"s_ps{jb}", tag="s_ps") for jb in range(NB)]
         for cb in range(CB):
             for name in "kqv":
@@ -68,45 +67,60 @@ def tile_neuromodulatedattentionwithelectrodes_kernel(tc, emb, q, k, v, offs, ou
                     start=(cb == 0),
                     stop=(cb == CB - 1),
                 )
-
-        veT = []
-        for cb in range(CB):
             veT_ps = flipped.tile([P, NB, P], F32, name="veT_ps", tag="flip")
             for ib in range(NB):
                 nc.tensor.transpose(veT_ps[:, ib, :], summed["v", cb][:, ib * P : (ib + 1) * P], identity32[:])
             veT.append(held.tile([P, NB, P], BF16, name=f"veT{cb}"))
             nc.scalar.copy(veT[cb][:], veT_ps[:])
 
+        mean_var, root, gain, shift, e, e_sum, p, pT_ps = {}, {}, {}, {}, {}, {}, {}, {}
         out_blocks = out.rearrange("(cb p) j -> p cb j", p=P)
-        for jb in range(NB):
-            stats = small.tile([P, 6], F32, name="stats")
+
+        def measure(jb):
+            stats = held.tile([P, 6], F32, name=f"stats{jb}")
             nc.vector.bn_stats(stats[:], s_ps[jb][:])
-            mean_var = small.tile([P, 2], F32, name="mean_var")
-            nc.vector.bn_aggr(mean_var[:], stats[:])
-            root = small.tile([P, 1], F32, name="root")
-            nc.gpsimd.tensor_tensor(root[:], mean_var[:, 1:2], half[:], POW)
-            gain = small.tile([P, 1], F32, name="gain")
-            nc.vector.tensor_scalar(gain[:], root[:], math.sqrt(N / (N - 1)), math.sqrt(C) * EPS, MULT, ADD)
-            nc.vector.reciprocal(gain[:], gain[:])
-            shift = small.tile([P, 1], F32, name="shift")
-            nc.vector.tensor_scalar(shift[:], mean_var[:, 0:1], gain[:], -1.0, MULT, MULT)
-            e = rows.tile([P, N], F32, name="e")
-            e_sum = small.tile([P, 1], F32, name="e_sum")
-            nc.scalar.activation(e[:], s_ps[jb][:], EXP, bias=shift[:], scale=gain[:], accum_out=e_sum[:])
-            nc.vector.reciprocal(e_sum[:], e_sum[:])
-            p = rows.tile([P, N], BF16, name="p")
-            nc.vector.tensor_scalar(p[:], e[:], e_sum[:], None, MULT)
-            pT_ps = flipped.tile([P, NB, P], BF16, name="pT_ps", tag="flip")
+            mean_var[jb] = held.tile([P, 2], F32, name=f"mean_var{jb}")
+            nc.vector.bn_aggr(mean_var[jb][:], stats[:])
+            root[jb] = held.tile([P, 1], F32, name=f"root{jb}")
+            nc.gpsimd.tensor_tensor(root[jb][:], mean_var[jb][:, 1:2], half[:], POW)
+
+        def exponentiate(jb):
+            gain[jb] = held.tile([P, 1], F32, name=f"gain{jb}")
+            nc.vector.tensor_scalar(
+                gain[jb][:], root[jb][:], math.sqrt(N / (N - 1)), math.sqrt(C) * EPS, MULT, ADD
+            )
+            nc.vector.reciprocal(gain[jb][:], gain[jb][:])
+            shift[jb] = held.tile([P, 1], F32, name=f"shift{jb}")
+            nc.vector.tensor_scalar(shift[jb][:], mean_var[jb][:, 0:1], gain[jb][:], -1.0, MULT, MULT)
+            e[jb] = held.tile([P, N], F32, name=f"e{jb}")
+            e_sum[jb] = held.tile([P, 1], F32, name=f"e_sum{jb}")
+            nc.scalar.activation(
+                e[jb][:], s_ps[jb][:], EXP, bias=shift[jb][:], scale=gain[jb][:], accum_out=e_sum[jb][:]
+            )
+
+        def normalise_and_flip(jb):
+            nc.vector.reciprocal(e_sum[jb][:], e_sum[jb][:])
+            p[jb] = held.tile([P, N], BF16, name=f"p{jb}")
+            nc.gpsimd.tensor_scalar(p[jb][:], e[jb][:], e_sum[jb][:], 1.0, MULT, MULT)
+            pT_ps[jb] = flipped.tile([P, NB, P], BF16, name=f"pT_ps{jb}", tag="flip")
             for ib in range(NB):
-                nc.tensor.transpose(pT_ps[:, ib, :], p[:, ib * P : (ib + 1) * P], identity16[:])
-            pT = rows.tile([P, NB, P], BF16, name="pT")
-            nc.scalar.copy(pT[:], pT_ps[:])
+                nc.tensor.transpose(pT_ps[jb][:, ib, :], p[jb][:, ib * P : (ib + 1) * P], identity16[:])
+
+        def weigh_and_store(jb):
+            pT = held.tile([P, NB, P], BF16, name=f"pT{jb}")
+            nc.vector.tensor_copy(pT[:], pT_ps[jb][:])
             o_ps = products.tile([P, CB, P], F32, name="o_ps")
             for cb in range(CB):
                 for ib in range(NB):
                     nc.tensor.matmul(
                         o_ps[:, cb, :], veT[cb][:, ib, :], pT[:, ib, :], start=(ib == 0), stop=(ib == NB - 1)
                     )
-            o = rows.tile([P, CB, P], F32, name="o")
+            o = held.tile([P, CB, P], F32, name=f"o{jb}")
             nc.scalar.copy(o[:], o_ps[:])
             nc.sync.dma_start(out_blocks[:, :, jb * P : (jb + 1) * P], o[:])
+
+        stages = (measure, exponentiate, normalise_and_flip, weigh_and_store)
+        for step in range(NB + len(stages) - 1):
+            for lag, stage in enumerate(stages):
+                if 0 <= step - lag < NB:
+                    stage(step - lag)

@@ -53,20 +53,28 @@ def tile_neuromodulatedattentionwithelectrodes_kernel(tc, emb, q, k, v, offs, ou
         for cb in range(CB):
             for name in "kqv":
                 summed[name, cb] = held.tile([P, N], F32, name=f"{name}e32_{cb}")
-                nc.vector.tensor_tensor(
-                    summed[name, cb][:], table[cb][:].indirect(offsets[:]), plain[name, cb][:], ADD
-                )
             for name in "kq":
                 rounded[name, cb] = held.tile([P, N], BF16, name=f"{name}e16_{cb}")
-                nc.scalar.copy(rounded[name, cb][:], summed[name, cb][:])
-            for jb in range(NB):
-                nc.tensor.matmul(
-                    s_ps[jb][:],
-                    rounded["q", cb][:, jb * P : (jb + 1) * P],
-                    rounded["k", cb][:],
-                    start=(cb == 0),
-                    stop=(cb == CB - 1),
+            nc.vector.tensor_tensor(summed["k", cb][:], table[cb][:].indirect(offsets[:]), plain["k", cb][:], ADD)
+            nc.scalar.copy(rounded["k", cb][:], summed["k", cb][:])
+            for first in range(0, N, N // 2):
+                columns = slice(first, first + N // 2)
+                nc.vector.tensor_tensor(
+                    summed["q", cb][:, columns],
+                    table[cb][:].indirect(offsets[:, first // 16 : (first + N // 2) // 16]),
+                    plain["q", cb][:, columns],
+                    ADD,
                 )
+                nc.scalar.copy(rounded["q", cb][:, columns], summed["q", cb][:, columns])
+                for jb in range(first // P, (first + N // 2) // P):
+                    nc.tensor.matmul(
+                        s_ps[jb][:],
+                        rounded["q", cb][:, jb * P : (jb + 1) * P],
+                        rounded["k", cb][:],
+                        start=(cb == 0),
+                        stop=(cb == CB - 1),
+                    )
+            nc.vector.tensor_tensor(summed["v", cb][:], table[cb][:].indirect(offsets[:]), plain["v", cb][:], ADD)
             veT_ps = flipped.tile([P, NB, P], F32, name="veT_ps", tag="flip")
             for ib in range(NB):
                 nc.tensor.transpose(veT_ps[:, ib, :], summed["v", cb][:, ib * P : (ib + 1) * P], identity32[:])
@@ -101,7 +109,7 @@ def tile_neuromodulatedattentionwithelectrodes_kernel(tc, emb, q, k, v, offs, ou
         def normalise_and_flip(jb):
             nc.vector.reciprocal(e_sum[jb][:], e_sum[jb][:])
             p[jb] = held.tile([P, N], BF16, name=f"p{jb}")
-            nc.gpsimd.tensor_scalar(p[jb][:], e[jb][:], e_sum[jb][:], 1.0, MULT, MULT)
+            nc.vector.tensor_scalar(p[jb][:], e[jb][:], e_sum[jb][:], None, MULT)
             pT_ps[jb] = flipped.tile([P, NB, P], BF16, name=f"pT_ps{jb}", tag="flip")
             for ib in range(NB):
                 nc.tensor.transpose(pT_ps[jb][:, ib, :], p[jb][:, ib * P : (ib + 1) * P], identity16[:])

@@ -34,8 +34,10 @@ def tile_neuromodulatedattentionwithelectrodes_kernel(tc, emb, q, k, v, offs, ou
         for cb in range(CB):
             channels = slice(cb * P, (cb + 1) * P)
             nc.sync.dma_start(table[cb][:], emb[channels, :])
-            for name, source in (("k", k), ("q", q), ("v", v)):
+            for name, source in (("k", k), ("q", q)):
                 nc.sync.dma_start(plain[name, cb][:], source[channels, :])
+        for cb in range(CB):
+            nc.sync.dma_start(plain["v", cb][:], v[cb * P : (cb + 1) * P, :])
 
         identity32 = held.tile([P, P], F32, name="identity32")
         make_identity(nc, identity32[:])
@@ -51,29 +53,24 @@ def tile_neuromodulatedattentionwithelectrodes_kernel(tc, emb, q, k, v, offs, ou
         veT = []
         s_ps = [scores.tile([P, N], F32, name=f"s_ps{jb}", tag="s_ps") for jb in range(NB)]
         for cb in range(CB):
-            for name in "kqv":
+            for name in "kq":
                 summed[name, cb] = held.tile([P, N], F32, name=f"{name}e32_{cb}")
+                nc.vector.tensor_tensor(
+                    summed[name, cb][:], table[cb][:].indirect(offsets[:]), plain[name, cb][:], ADD
+                )
             for name in "kq":
                 rounded[name, cb] = held.tile([P, N], BF16, name=f"{name}e16_{cb}")
-            nc.vector.tensor_tensor(summed["k", cb][:], table[cb][:].indirect(offsets[:]), plain["k", cb][:], ADD)
-            nc.scalar.copy(rounded["k", cb][:], summed["k", cb][:])
-            for first in range(0, N, N // 2):
-                columns = slice(first, first + N // 2)
-                nc.vector.tensor_tensor(
-                    summed["q", cb][:, columns],
-                    table[cb][:].indirect(offsets[:, first // 16 : (first + N // 2) // 16]),
-                    plain["q", cb][:, columns],
-                    ADD,
+                nc.scalar.copy(rounded[name, cb][:], summed[name, cb][:])
+            for jb in range(NB):
+                nc.tensor.matmul(
+                    s_ps[jb][:],
+                    rounded["q", cb][:, jb * P : (jb + 1) * P],
+                    rounded["k", cb][:],
+                    start=(cb == 0),
+                    stop=(cb == CB - 1),
                 )
-                nc.scalar.copy(rounded["q", cb][:, columns], summed["q", cb][:, columns])
-                for jb in range(first // P, (first + N // 2) // P):
-                    nc.tensor.matmul(
-                        s_ps[jb][:],
-                        rounded["q", cb][:, jb * P : (jb + 1) * P],
-                        rounded["k", cb][:],
-                        start=(cb == 0),
-                        stop=(cb == CB - 1),
-                    )
+        for cb in range(CB):
+            summed["v", cb] = held.tile([P, N], F32, name=f"ve32_{cb}")
             nc.vector.tensor_tensor(summed["v", cb][:], table[cb][:].indirect(offsets[:]), plain["v", cb][:], ADD)
             veT_ps = flipped.tile([P, NB, P], F32, name="veT_ps", tag="flip")
             for ib in range(NB):

@@ -78,6 +78,10 @@ def tile_neuromodulatedattentionwithelectrodes_kernel(tc, emb, q, k, v, offs, ou
             veT.append(held.tile([P, NB, P], BF16, name=f"veT{cb}"))
             nc.scalar.copy(veT[cb][:], veT_ps[:])
 
+        idle_ps = products.tile([P, N], F32, name="idle_ps", tag="o_ps")
+        for repeat in range(12):
+            nc.tensor.matmul(idle_ps[:], identity16[:], rounded["k", CB - 1][:], start=True, stop=True)
+
         mean_var, root, gain, shift, e, e_sum, p, pT_ps = {}, {}, {}, {}, {}, {}, {}, {}
         out_blocks = out.rearrange("(cb p) j -> p cb j", p=P)
 

@@ -128,8 +128,6 @@ def tile_neuromodulatedattentionwithelectrodes_kernel(tc, emb, q, k, v, offs, ou
             nc.scalar.copy(o[:], o_ps[:])
             nc.sync.dma_start(out_blocks[:, :, jb * P : (jb + 1) * P], o[:])
 
-        stages = (measure, exponentiate, normalise_and_flip, weigh_and_store)
-        for step in range(NB + len(stages) - 1):
-            for lag, stage in enumerate(stages):
-                if 0 <= step - lag < NB:
-                    stage(step - lag)
+        for stage in (measure, exponentiate, normalise_and_flip, weigh_and_store):
+            for jb in range(NB):
+                stage(jb)

@@ -7,6 +7,8 @@ P = 128
 C, S, N = 256, 2048, 512
 CB = C // P
 NB = N // P
+HALVES = 2
+HB = NB // HALVES
 EPS = 1e-6
 
 FLOPS = 2 * 2 * N * N * C
@@ -22,8 +24,7 @@ def tile_neuromodulatedattentionwithelectrodes_kernel(tc, emb, q, k, v, offs, ou
     with (
         tc.tile_pool(name="held", bufs=1) as held,
         tc.psum_pool(name="scores", bufs=NB) as scores,
-        tc.psum_pool(name="flipped", bufs=2) as flipped,
-        tc.psum_pool(name="products", bufs=2) as products,
+        tc.psum_pool(name="flipped", bufs=NB) as flipped,
     ):
         offsets = held.tile([P, N // 16], U16, name="offsets")
         nc.sync.dma_start(offsets[:], offs)
@@ -78,7 +79,7 @@ def tile_neuromodulatedattentionwithelectrodes_kernel(tc, emb, q, k, v, offs, ou
             veT.append(held.tile([P, NB, P], BF16, name=f"veT{cb}"))
             nc.scalar.copy(veT[cb][:], veT_ps[:])
 
-        idle_ps = products.tile([P, N], F32, name="idle_ps", tag="o_ps")
+        idle_ps = flipped.tile([P, N], F32, name="idle_ps", tag="flip")
         for repeat in range(12):
             nc.tensor.matmul(idle_ps[:], identity16[:], rounded["k", CB - 1][:], start=True, stop=True)
 
@@ -111,21 +112,26 @@ def tile_neuromodulatedattentionwithelectrodes_kernel(tc, emb, q, k, v, offs, ou
             nc.vector.reciprocal(e_sum[jb][:], e_sum[jb][:])
             p[jb] = held.tile([P, N], BF16, name=f"p{jb}")
             nc.vector.tensor_scalar(p[jb][:], e[jb][:], e_sum[jb][:], None, MULT)
-            pT_ps[jb] = flipped.tile([P, NB, P], BF16, name=f"pT_ps{jb}", tag="flip")
-            for ib in range(NB):
-                nc.tensor.transpose(pT_ps[jb][:, ib, :], p[jb][:, ib * P : (ib + 1) * P], identity16[:])
+            for h in range(HALVES):
+                pT_ps[jb, h] = flipped.tile([P, HB, P], BF16, name=f"pT_ps{jb}_{h}", tag="flip")
+                for hb in range(HB):
+                    ib = h * HB + hb
+                    nc.tensor.transpose(pT_ps[jb, h][:, hb, :], p[jb][:, ib * P : (ib + 1) * P], identity16[:])
 
         def weigh_and_store(jb):
-            pT = held.tile([P, NB, P], BF16, name=f"pT{jb}")
-            nc.vector.tensor_copy(pT[:], pT_ps[jb][:])
-            o_ps = products.tile([P, CB, P], F32, name="o_ps")
-            for cb in range(CB):
-                for ib in range(NB):
-                    nc.tensor.matmul(
-                        o_ps[:, cb, :], veT[cb][:, ib, :], pT[:, ib, :], start=(ib == 0), stop=(ib == NB - 1)
-                    )
+            o_ps = [scores.tile([P, P], F32, name=f"o_ps{jb}_{cb}", tag="s_ps") for cb in range(CB)]
+            for h in range(HALVES):
+                pT = held.tile([P, HB, P], BF16, name=f"pT{jb}_{h}")
+                nc.vector.tensor_copy(pT[:], pT_ps[jb, h][:])
+                for cb in range(CB):
+                    for hb in range(HB):
+                        ib = h * HB + hb
+                        nc.tensor.matmul(
+                            o_ps[cb][:], veT[cb][:, ib, :], pT[:, hb, :], start=(ib == 0), stop=(ib == NB - 1)
+                        )
             o = held.tile([P, CB, P], F32, name=f"o{jb}")
-            nc.scalar.copy(o[:], o_ps[:])
+            for cb in range(CB):
+                nc.scalar.copy(o[:, cb, :], o_ps[cb][:])
             nc.sync.dma_start(out_blocks[:, :, jb * P : (jb + 1) * P], o[:])
 
         for stage in (measure, exponentiate, normalise_and_flip, weigh_and_store):

@@ -122,7 +122,10 @@ def tile_neuromodulatedattentionwithelectrodes_kernel(tc, emb, q, k, v, offs, ou
             o_ps = [scores.tile([P, P], F32, name=f"o_ps{jb}_{cb}", tag="s_ps") for cb in range(CB)]
             for h in range(HALVES):
                 pT = held.tile([P, HB, P], BF16, name=f"pT{jb}_{h}")
-                nc.vector.tensor_copy(pT[:], pT_ps[jb, h][:])
+                if h == 0:
+                    nc.vector.tensor_copy(pT[:], pT_ps[jb, h][:])
+                else:
+                    nc.scalar.copy(pT[:], pT_ps[jb, h][:])
                 for cb in range(CB):
                     for hb in range(HB):
                         ib = h * HB + hb

@@ -119,22 +119,23 @@ def tile_neuromodulatedattentionwithelectrodes_kernel(tc, emb, q, k, v, offs, ou
                     nc.tensor.transpose(pT_ps[jb, h][:, hb, :], p[jb][:, ib * P : (ib + 1) * P], identity16[:])
 
         def weigh_and_store(jb):
-            o_ps = [scores.tile([P, P], F32, name=f"o_ps{jb}_{cb}", tag="s_ps") for cb in range(CB)]
+            pT = {}
             for h in range(HALVES):
-                pT = held.tile([P, HB, P], BF16, name=f"pT{jb}_{h}")
-                if h == 0:
-                    nc.vector.tensor_copy(pT[:], pT_ps[jb, h][:])
-                else:
-                    nc.scalar.copy(pT[:], pT_ps[jb, h][:])
-                for cb in range(CB):
-                    for hb in range(HB):
-                        ib = h * HB + hb
-                        nc.tensor.matmul(
-                            o_ps[cb][:], veT[cb][:, ib, :], pT[:, hb, :], start=(ib == 0), stop=(ib == NB - 1)
-                        )
-            o = held.tile([P, CB, P], F32, name=f"o{jb}")
+                pT[h] = held.tile([P, HB, P], BF16, name=f"pT{jb}_{h}")
+            nc.vector.tensor_copy(pT[0][:], pT_ps[jb, 0][:])
+            nc.scalar.copy(pT[1][:], pT_ps[jb, 1][:])
+            o_ps = scores.tile([P, CB, P], F32, name=f"o_ps{jb}", tag="s_ps")
             for cb in range(CB):
-                nc.scalar.copy(o[:, cb, :], o_ps[cb][:])
+                for ib in range(NB):
+                    nc.tensor.matmul(
+                        o_ps[:, cb, :],
+                        veT[cb][:, ib, :],
+                        pT[ib // HB][:, ib % HB, :],
+                        start=(ib == 0),
+                        stop=(ib == NB - 1),
+                    )
+            o = held.tile([P, CB, P], F32, name=f"o{jb}")
+            nc.scalar.copy(o[:], o_ps[:])
             nc.sync.dma_start(out_blocks[:, :, jb * P : (jb + 1) * P], o[:])
 
         for stage in (measure, exponentiate, normalise_and_flip, weigh_and_store):

import math

import concourse.mybir as mybir
from concourse.masks import make_identity

P = 128
C, S, N = 256, 2048, 512
CB = C // P
NB = N // P
HALVES = 2
HB = NB // HALVES
EPS = 1e-6

FLOPS = 2 * 2 * N * N * C
BYTES = 4 * (C * N + 3 * C * N + C * N) + 2 * P * (N // 16)

F32, BF16, U16 = mybir.dt.float32, mybir.dt.bfloat16, mybir.dt.uint16
ADD, MULT, POW = mybir.AluOpType.add, mybir.AluOpType.mult, mybir.AluOpType.pow
EXP = mybir.ActivationFunctionType.Exp


def tile_neuromodulatedattentionwithelectrodes_kernel(tc, emb, q, k, v, offs, out):
    nc = tc.nc
    with (
        tc.tile_pool(name="held", bufs=1) as held,
        tc.psum_pool(name="scores", bufs=NB) as scores,
        tc.psum_pool(name="flipped", bufs=NB) as flipped,
    ):
        offsets = held.tile([P, N // 16], U16, name="offsets")
        nc.sync.dma_start(offsets[:], offs)
        table = [held.tile([P, S], F32, name=f"table{cb}") for cb in range(CB)]
        plain = {
            (name, cb): held.tile([P, N], F32, name=f"{name}{cb}") for name in "kqv" for cb in range(CB)
        }
        for cb in range(CB):
            channels = slice(cb * P, (cb + 1) * P)
            nc.sync.dma_start(table[cb][:], emb[channels, :])
            for name, source in (("k", k), ("q", q)):
                nc.sync.dma_start(plain[name, cb][:], source[channels, :])
        for cb in range(CB):
            nc.sync.dma_start(plain["v", cb][:], v[cb * P : (cb + 1) * P, :])

        identity32 = held.tile([P, P], F32, name="identity32")
        make_identity(nc, identity32[:])
        identity16 = held.tile([P, P], BF16, name="identity16")
        make_identity(nc, identity16[:])
        half = held.tile([P, 1], F32, name="half")
        nc.gpsimd.memset(half[:], 0.5)
        warm = held.tile([P, 1], F32, name="warm")
        nc.scalar.activation(warm[:], half[:], EXP)

        summed = {}
        rounded = {}
        veT = []
        s_ps = [scores.tile([P, N], F32, name=f"s_ps{jb}", tag="s_ps") for jb in range(NB)]
        for cb in range(CB):
            for name in "kq":
                summed[name, cb] = held.tile([P, N], F32, name=f"{name}e32_{cb}")
                nc.vector.tensor_tensor(
                    summed[name, cb][:], table[cb][:].indirect(offsets[:]), plain[name, cb][:], ADD
                )
            for name in "kq":
                rounded[name, cb] = held.tile([P, N], BF16, name=f"{name}e16_{cb}")
                nc.scalar.copy(rounded[name, cb][:], summed[name, cb][:])
            for jb in range(NB):
                nc.tensor.matmul(
                    s_ps[jb][:],
                    rounded["q", cb][:, jb * P : (jb + 1) * P],
                    rounded["k", cb][:],
                    start=(cb == 0),
                    stop=(cb == CB - 1),
                )
        for cb in range(CB):
            summed["v", cb] = held.tile([P, N], F32, name=f"ve32_{cb}")
            nc.vector.tensor_tensor(summed["v", cb][:], table[cb][:].indirect(offsets[:]), plain["v", cb][:], ADD)
            veT_ps = flipped.tile([P, NB, P], F32, name="veT_ps", tag="flip")
            for ib in range(NB):
                nc.tensor.transpose(veT_ps[:, ib, :], summed["v", cb][:, ib * P : (ib + 1) * P], identity32[:])
            veT.append(held.tile([P, NB, P], BF16, name=f"veT{cb}"))
            nc.scalar.copy(veT[cb][:], veT_ps[:])

        idle_ps = flipped.tile([P, N], F32, name="idle_ps", tag="flip")
        for repeat in range(12):
            nc.tensor.matmul(idle_ps[:], identity16[:], rounded["k", CB - 1][:], start=True, stop=True)

        mean_var, root, gain, shift, e, e_sum, p, pT_ps = {}, {}, {}, {}, {}, {}, {}, {}
        out_blocks = out.rearrange("(cb p) j -> p cb j", p=P)

        def measure(jb):
            stats = held.tile([P, 6], F32, name=f"stats{jb}")
            nc.vector.bn_stats(stats[:], s_ps[jb][:])
            mean_var[jb] = held.tile([P, 2], F32, name=f"mean_var{jb}")
            nc.vector.bn_aggr(mean_var[jb][:], stats[:])
            root[jb] = held.tile([P, 1], F32, name=f"root{jb}")
            nc.gpsimd.tensor_tensor(root[jb][:], mean_var[jb][:, 1:2], half[:], POW)

        def exponentiate(jb):
            gain[jb] = held.tile([P, 1], F32, name=f"gain{jb}")
            nc.vector.tensor_scalar(
                gain[jb][:], root[jb][:], math.sqrt(N / (N - 1)), math.sqrt(C) * EPS, MULT, ADD
            )
            nc.vector.reciprocal(gain[jb][:], gain[jb][:])
            shift[jb] = held.tile([P, 1], F32, name=f"shift{jb}")
            nc.vector.tensor_scalar(shift[jb][:], mean_var[jb][:, 0:1], gain[jb][:], -1.0, MULT, MULT)
            e[jb] = held.tile([P, N], F32, name=f"e{jb}")
            e_sum[jb] = held.tile([P, 1], F32, name=f"e_sum{jb}")
            nc.scalar.activation(
                e[jb][:], s_ps[jb][:], EXP, bias=shift[jb][:], scale=gain[jb][:], accum_out=e_sum[jb][:]
            )

        def normalise_and_flip(jb):
            nc.vector.reciprocal(e_sum[jb][:], e_sum[jb][:])
            p[jb] = held.tile([P, N], BF16, name=f"p{jb}")
            nc.vector.tensor_scalar(p[jb][:], e[jb][:], e_sum[jb][:], None, MULT)
            for h in range(HALVES):
                pT_ps[jb, h] = flipped.tile([P, HB, P], BF16, name=f"pT_ps{jb}_{h}", tag="flip")
                for hb in range(HB):
                    ib = h * HB + hb
                    nc.tensor.transpose(pT_ps[jb, h][:, hb, :], p[jb][:, ib * P : (ib + 1) * P], identity16[:])

        def weigh_and_store(jb):
            pT = {}
            for h in range(HALVES):
                pT[h] = held.tile([P, HB, P], BF16, name=f"pT{jb}_{h}")
            nc.vector.tensor_copy(pT[0][:], pT_ps[jb, 0][:])
            nc.scalar.copy(pT[1][:], pT_ps[jb, 1][:])
            o_ps = scores.tile([P, CB, P], F32, name=f"o_ps{jb}", tag="s_ps")
            for cb in range(CB):
                for ib in range(NB):
                    nc.tensor.matmul(
                        o_ps[:, cb, :],
                        veT[cb][:, ib, :],
                        pT[ib // HB][:, ib % HB, :],
                        start=(ib == 0),
                        stop=(ib == NB - 1),
                    )
            o = held.tile([P, CB, P], F32, name=f"o{jb}")
            nc.scalar.copy(o[:], o_ps[:])
            nc.sync.dma_start(out_blocks[:, :, jb * P : (jb + 1) * P], o[:])

        for stage in (measure, exponentiate, normalise_and_flip, weigh_and_store):
            for jb in range(NB):
                stage(jb)
